import numpy as np
import ml_dtypes

BF16 = ml_dtypes.bfloat16


def bf(x):
    return np.asarray(x, np.float32).astype(BF16)


def f32(x):
    return np.asarray(x, np.float32)


def f64(x):
    return np.asarray(x).astype(np.float64)


def striped(idx):
    return np.tile(idx.reshape(-1, 16).T, (8, 1))


C, K, S, N = 256, 256, 512, 256
W_STD = 0.5


def setup_inputs():
    return {"base": f32(np.random.standard_normal((C, S))), "x": bf(np.random.standard_normal((K, N))), "w": bf(W_STD * np.random.standard_normal((C, K)) / np.sqrt(K)), "bias": f32(0.1 * np.random.standard_normal((C, 1))), "mag": f32(1.0 + 0.1 * np.random.standard_normal((C, 1))), "offs": striped(np.random.permutation(S)[:N])}


def reference(base, x, w, bias, mag, offs):
    idx = offs[:16].T.reshape(-1)
    wn = np.sqrt(np.sum(f64(w) ** 2, axis=1, keepdims=True))
    scale = f64(mag) / wn
    y = (scale - 1.0) * (f64(w) @ f64(x) + f64(bias))
    out = f64(base).copy()
    out[:, idx] = y
    return out

@@ -1,0 +1,65 @@
+import concourse.mybir as mybir
+from concourse.masks import make_identity
+
+P = 128
+C, K, S, N = 256, 256, 512, 256
+CB = C // P
+KB = K // P
+FLOPS = 2 * C * K * N
+
+BF16, F32, U16 = mybir.dt.bfloat16, mybir.dt.float32, mybir.dt.uint16
+ADD, MULT = mybir.AluOpType.add, mybir.AluOpType.mult
+COPY, SQRT = mybir.ActivationFunctionType.Copy, mybir.ActivationFunctionType.Sqrt
+
+
+def tile_relaxedrecursivedoralinear_kernel(tc, base, x, w, bias, mag, offs, out):
+    nc = tc.nc
+    with tc.tile_pool(name="held", bufs=1) as held, tc.psum_pool(name="psum", bufs=1) as psum:
+        w_rows = held.tile([P, CB, K], BF16, name="w_rows")
+        nc.sync.dma_start(w_rows[:], w.rearrange("(cb p) k -> p cb k", p=P))
+        x_rows = held.tile([P, KB, N], BF16, name="x_rows")
+        nc.scalar.dma_start(x_rows[:], x.rearrange("(kb p) n -> p kb n", p=P))
+        offsets = held.tile([P, N // 16], U16, name="offsets")
+        nc.sync.dma_start(offsets[:], offs)
+        windows = [held.tile([P, S], F32, name=f"window{cb}") for cb in range(CB)]
+        for cb in range(CB):
+            nc.sync.dma_start(windows[cb][:], base[cb * P : (cb + 1) * P, :])
+        bias_cols = held.tile([P, CB], F32, name="bias_cols")
+        mag_cols = held.tile([P, CB], F32, name="mag_cols")
+        with nc.allow_non_contiguous_dma(reason="256 single float32 values, one to a partition and block"):
+            nc.scalar.dma_start(bias_cols[:], bias.rearrange("(cb p) o -> p (cb o)", p=P))
+            nc.scalar.dma_start(mag_cols[:], mag.rearrange("(cb p) o -> p (cb o)", p=P))
+
+        identity = held.tile([P, P], BF16, name="identity")
+        make_identity(nc, identity[:])
+
+        squares = held.tile([P, CB, K], F32, name="squares")
+        nc.vector.tensor_tensor(squares[:], w_rows[:], w_rows[:], MULT)
+        gain = held.tile([P, CB], F32, name="gain")
+        nc.vector.reduce_sum(gain[:], squares[:], axis=mybir.AxisListType.X)
+        nc.scalar.activation(gain[:], gain[:], SQRT)
+        nc.vector.reciprocal(gain[:], gain[:])
+        nc.vector.tensor_tensor(gain[:], gain[:], mag_cols[:], MULT)
+        nc.vector.tensor_scalar_add(gain[:], gain[:], -1.0)
+
+        flipped = []
+        for cb in range(CB):
+            flip_psum = psum.tile([P, KB, P], BF16, name=f"flip_psum{cb}")
+            for kb in range(KB):
+                nc.tensor.transpose(flip_psum[:, kb, :], w_rows[:, cb, kb * P : (kb + 1) * P], identity[:])
+            flipped.append(held.tile([P, KB, P], BF16, name=f"flipped{cb}"))
+            nc.scalar.activation(flipped[cb][:], flip_psum[:], COPY)
+
+        finished = []
+        for cb in range(CB):
+            product = psum.tile([P, N], F32, name=f"product{cb}")
+            for kb in range(KB):
+                nc.tensor.matmul(product[:], flipped[cb][:, kb, :], x_rows[:, kb, :], start=kb == 0, stop=kb == KB - 1)
+            finished.append(held.tile([P, N], F32, name=f"finished{cb}"))
+            nc.vector.tensor_scalar(
+                finished[cb][:], product[:], bias_cols[:, cb : cb + 1], gain[:, cb : cb + 1], op0=ADD, op1=MULT
+            )
+
+        for cb in range(CB):
+            nc.scalar.activation(windows[cb][:].indirect(offsets[:]), finished[cb][:], COPY)
+            nc.sync.dma_start(out[cb * P : (cb + 1) * P, :], windows[cb][:])

@@ -19,43 +19,49 @@ def tile_relaxedrecursivedoralinear_kernel(tc, base, x, w, bias, mag, offs, out)
         nc.sync.dma_start(w_rows[:], w.rearrange("(cb p) k -> p cb k", p=P))
         x_rows = held.tile([P, KB, N], BF16, name="x_rows")
         nc.scalar.dma_start(x_rows[:], x.rearrange("(kb p) n -> p kb n", p=P))
+        bias_cols = held.tile([P, CB], F32, name="bias_cols")
+        mag_cols = held.tile([P, CB], F32, name="mag_cols")
+        with nc.allow_non_contiguous_dma(reason="256 single float32 values, one to a partition and block"):
+            nc.sync.dma_start(mag_cols[:], mag.rearrange("(cb p) o -> p (cb o)", p=P))
+            nc.sync.dma_start(bias_cols[:], bias.rearrange("(cb p) o -> p (cb o)", p=P))
         offsets = held.tile([P, N // 16], U16, name="offsets")
         nc.sync.dma_start(offsets[:], offs)
         windows = [held.tile([P, S], F32, name=f"window{cb}") for cb in range(CB)]
         for cb in range(CB):
             nc.sync.dma_start(windows[cb][:], base[cb * P : (cb + 1) * P, :])
-        bias_cols = held.tile([P, CB], F32, name="bias_cols")
-        mag_cols = held.tile([P, CB], F32, name="mag_cols")
-        with nc.allow_non_contiguous_dma(reason="256 single float32 values, one to a partition and block"):
-            nc.scalar.dma_start(bias_cols[:], bias.rearrange("(cb p) o -> p (cb o)", p=P))
-            nc.scalar.dma_start(mag_cols[:], mag.rearrange("(cb p) o -> p (cb o)", p=P))
 
         identity = held.tile([P, P], BF16, name="identity")
         make_identity(nc, identity[:])
 
-        squares = held.tile([P, CB, K], F32, name="squares")
-        nc.vector.tensor_tensor(squares[:], w_rows[:], w_rows[:], MULT)
-        gain = held.tile([P, CB], F32, name="gain")
-        nc.vector.reduce_sum(gain[:], squares[:], axis=mybir.AxisListType.X)
-        nc.scalar.activation(gain[:], gain[:], SQRT)
-        nc.vector.reciprocal(gain[:], gain[:])
-        nc.vector.tensor_tensor(gain[:], gain[:], mag_cols[:], MULT)
-        nc.vector.tensor_scalar_add(gain[:], gain[:], -1.0)
-
-        flipped = []
+        flip_psum = [psum.tile([P, KB, P], BF16, name=f"flip_psum{cb}") for cb in range(CB)]
+        flipped = [held.tile([P, KB, P], BF16, name=f"flipped{cb}") for cb in range(CB)]
         for cb in range(CB):
-            flip_psum = psum.tile([P, KB, P], BF16, name=f"flip_psum{cb}")
             for kb in range(KB):
-                nc.tensor.transpose(flip_psum[:, kb, :], w_rows[:, cb, kb * P : (kb + 1) * P], identity[:])
-            flipped.append(held.tile([P, KB, P], BF16, name=f"flipped{cb}"))
-            nc.scalar.activation(flipped[cb][:], flip_psum[:], COPY)
+                nc.tensor.transpose(flip_psum[cb][:, kb, :], w_rows[:, cb, kb * P : (kb + 1) * P], identity[:])
+        nc.scalar.activation(flipped[0][:], flip_psum[0][:], COPY)
 
-        finished = []
+        sumsq = held.tile([P, CB], F32, name="sumsq")
+        squares = held.tile([P, K], F32, name="squares")
+        for cb in range(CB):
+            nc.vector.scalar_tensor_tensor(
+                squares[:], w_rows[:, cb, :], 1.0, w_rows[:, cb, :], op0=MULT, op1=MULT, accum_out=sumsq[:, cb : cb + 1]
+            )
+        nc.vector.tensor_copy(flipped[1][:], flip_psum[1][:])
+        norm = held.tile([P, CB], F32, name="norm")
+        nc.scalar.activation(norm[:], sumsq[:], SQRT)
+        inv_norm = held.tile([P, CB], F32, name="inv_norm")
+        nc.vector.reciprocal(inv_norm[:], norm[:])
+        gain = held.tile([P, CB], F32, name="gain")
+        for cb in range(CB):
+            nc.vector.tensor_scalar(
+                gain[:, cb : cb + 1], inv_norm[:, cb : cb + 1], mag_cols[:, cb : cb + 1], -1.0, op0=MULT, op1=ADD
+            )
+
+        finished = [held.tile([P, N], F32, name=f"finished{cb}") for cb in range(CB)]
         for cb in range(CB):
             product = psum.tile([P, N], F32, name=f"product{cb}")
             for kb in range(KB):
                 nc.tensor.matmul(product[:], flipped[cb][:, kb, :], x_rows[:, kb, :], start=kb == 0, stop=kb == KB - 1)
-            finished.append(held.tile([P, N], F32, name=f"finished{cb}"))
             nc.vector.tensor_scalar(
                 finished[cb][:], product[:], bias_cols[:, cb : cb + 1], gain[:, cb : cb + 1], op0=ADD, op1=MULT
             )

@@ -11,6 +11,8 @@ BF16, F32, U16 = mybir.dt.bfloat16, mybir.dt.float32, mybir.dt.uint16
 ADD, MULT = mybir.AluOpType.add, mybir.AluOpType.mult
 COPY, SQRT = mybir.ActivationFunctionType.Copy, mybir.ActivationFunctionType.Sqrt
 
+WARM_COLS = 512
+WARM_MATMULS = 4
 
 def tile_relaxedrecursivedoralinear_kernel(tc, base, x, w, bias, mag, offs, out):
     nc = tc.nc
@@ -32,6 +34,12 @@ def tile_relaxedrecursivedoralinear_kernel(tc, base, x, w, bias, mag, offs, out)
 
         identity = held.tile([P, P], BF16, name="identity")
         make_identity(nc, identity[:])
+
+        zeros = held.tile([P, WARM_COLS], BF16, name="zeros")
+        nc.vector.memset(zeros[:], 0.0)
+        warm_psum = psum.tile([P, WARM_COLS], F32, name="warm_psum")
+        for i in range(WARM_MATMULS):
+            nc.tensor.matmul(warm_psum[:], zeros[:, :P], zeros[:], start=True, stop=True)
 
         flip_psum = [psum.tile([P, KB, P], BF16, name=f"flip_psum{cb}") for cb in range(CB)]
         flipped = [held.tile([P, KB, P], BF16, name=f"flipped{cb}") for cb in range(CB)]

@@ -11,48 +11,50 @@ BF16, F32, U16 = mybir.dt.bfloat16, mybir.dt.float32, mybir.dt.uint16
 ADD, MULT = mybir.AluOpType.add, mybir.AluOpType.mult
 COPY, SQRT = mybir.ActivationFunctionType.Copy, mybir.ActivationFunctionType.Sqrt
 
-WARM_COLS = 512
-WARM_MATMULS = 4
+WARM_MATMULS = 18
+
 
 def tile_relaxedrecursivedoralinear_kernel(tc, base, x, w, bias, mag, offs, out):
     nc = tc.nc
     with tc.tile_pool(name="held", bufs=1) as held, tc.psum_pool(name="psum", bufs=1) as psum:
-        w_rows = held.tile([P, CB, K], BF16, name="w_rows")
-        nc.sync.dma_start(w_rows[:], w.rearrange("(cb p) k -> p cb k", p=P))
+
+        zeros = held.tile([P, P], BF16, name="zeros")
+        nc.gpsimd.memset(zeros[:], 0.0)
+        warm_psum = psum.tile([P, P], F32, name="warm_psum")
+        for i in range(WARM_MATMULS):
+            nc.tensor.matmul(warm_psum[:], zeros[:], zeros[:], start=True, stop=True)
+
+        identity = held.tile([P, P], BF16, name="identity")
+        make_identity(nc, identity[:])
+
+        w_rows = [held.tile([P, K], BF16, name=f"w_rows{cb}") for cb in range(CB)]
+        for cb in range(CB):
+            nc.sync.dma_start(w_rows[cb][:], w[cb * P : (cb + 1) * P, :])
         x_rows = held.tile([P, KB, N], BF16, name="x_rows")
-        nc.scalar.dma_start(x_rows[:], x.rearrange("(kb p) n -> p kb n", p=P))
-        bias_cols = held.tile([P, CB], F32, name="bias_cols")
-        mag_cols = held.tile([P, CB], F32, name="mag_cols")
-        with nc.allow_non_contiguous_dma(reason="256 single float32 values, one to a partition and block"):
-            nc.sync.dma_start(mag_cols[:], mag.rearrange("(cb p) o -> p (cb o)", p=P))
-            nc.sync.dma_start(bias_cols[:], bias.rearrange("(cb p) o -> p (cb o)", p=P))
+        nc.sync.dma_start(x_rows[:], x.rearrange("(kb p) n -> p kb n", p=P))
         offsets = held.tile([P, N // 16], U16, name="offsets")
         nc.sync.dma_start(offsets[:], offs)
         windows = [held.tile([P, S], F32, name=f"window{cb}") for cb in range(CB)]
         for cb in range(CB):
             nc.sync.dma_start(windows[cb][:], base[cb * P : (cb + 1) * P, :])
-
-        identity = held.tile([P, P], BF16, name="identity")
-        make_identity(nc, identity[:])
-
-        zeros = held.tile([P, WARM_COLS], BF16, name="zeros")
-        nc.vector.memset(zeros[:], 0.0)
-        warm_psum = psum.tile([P, WARM_COLS], F32, name="warm_psum")
-        for i in range(WARM_MATMULS):
-            nc.tensor.matmul(warm_psum[:], zeros[:, :P], zeros[:], start=True, stop=True)
+        bias_cols = held.tile([P, CB], F32, name="bias_cols")
+        mag_cols = held.tile([P, CB], F32, name="mag_cols")
+        with nc.allow_non_contiguous_dma(reason="256 single float32 values, one to a partition and block"):
+            nc.scalar.dma_start(mag_cols[:], mag.rearrange("(cb p) o -> p (cb o)", p=P))
+            nc.scalar.dma_start(bias_cols[:], bias.rearrange("(cb p) o -> p (cb o)", p=P))
 
         flip_psum = [psum.tile([P, KB, P], BF16, name=f"flip_psum{cb}") for cb in range(CB)]
         flipped = [held.tile([P, KB, P], BF16, name=f"flipped{cb}") for cb in range(CB)]
         for cb in range(CB):
             for kb in range(KB):
-                nc.tensor.transpose(flip_psum[cb][:, kb, :], w_rows[:, cb, kb * P : (kb + 1) * P], identity[:])
+                nc.tensor.transpose(flip_psum[cb][:, kb, :], w_rows[cb][:, kb * P : (kb + 1) * P], identity[:])
         nc.scalar.activation(flipped[0][:], flip_psum[0][:], COPY)
 
         sumsq = held.tile([P, CB], F32, name="sumsq")
         squares = held.tile([P, K], F32, name="squares")
         for cb in range(CB):
             nc.vector.scalar_tensor_tensor(
-                squares[:], w_rows[:, cb, :], 1.0, w_rows[:, cb, :], op0=MULT, op1=MULT, accum_out=sumsq[:, cb : cb + 1]
+                squares[:], w_rows[cb][:], 1.0, w_rows[cb][:], op0=MULT, op1=MULT, accum_out=sumsq[:, cb : cb + 1]
             )
         nc.vector.tensor_copy(flipped[1][:], flip_psum[1][:])
         norm = held.tile([P, CB], F32, name="norm")

@@ -27,34 +27,33 @@ def tile_relaxedrecursivedoralinear_kernel(tc, base, x, w, bias, mag, offs, out)
         identity = held.tile([P, P], BF16, name="identity")
         make_identity(nc, identity[:])
 
-        w_rows = [held.tile([P, K], BF16, name=f"w_rows{cb}") for cb in range(CB)]
-        for cb in range(CB):
-            nc.sync.dma_start(w_rows[cb][:], w[cb * P : (cb + 1) * P, :])
+        w_rows = held.tile([P, CB, K], BF16, name="w_rows")
+        nc.sync.dma_start(w_rows[:], w.rearrange("(cb p) k -> p cb k", p=P))
         x_rows = held.tile([P, KB, N], BF16, name="x_rows")
-        nc.sync.dma_start(x_rows[:], x.rearrange("(kb p) n -> p kb n", p=P))
+        nc.scalar.dma_start(x_rows[:], x.rearrange("(kb p) n -> p kb n", p=P))
+        bias_cols = held.tile([P, CB], F32, name="bias_cols")
+        mag_cols = held.tile([P, CB], F32, name="mag_cols")
+        with nc.allow_non_contiguous_dma(reason="256 single float32 values, one to a partition and block"):
+            nc.sync.dma_start(mag_cols[:], mag.rearrange("(cb p) o -> p (cb o)", p=P))
+            nc.sync.dma_start(bias_cols[:], bias.rearrange("(cb p) o -> p (cb o)", p=P))
         offsets = held.tile([P, N // 16], U16, name="offsets")
         nc.sync.dma_start(offsets[:], offs)
         windows = [held.tile([P, S], F32, name=f"window{cb}") for cb in range(CB)]
         for cb in range(CB):
             nc.sync.dma_start(windows[cb][:], base[cb * P : (cb + 1) * P, :])
-        bias_cols = held.tile([P, CB], F32, name="bias_cols")
-        mag_cols = held.tile([P, CB], F32, name="mag_cols")
-        with nc.allow_non_contiguous_dma(reason="256 single float32 values, one to a partition and block"):
-            nc.scalar.dma_start(mag_cols[:], mag.rearrange("(cb p) o -> p (cb o)", p=P))
-            nc.scalar.dma_start(bias_cols[:], bias.rearrange("(cb p) o -> p (cb o)", p=P))
 
         flip_psum = [psum.tile([P, KB, P], BF16, name=f"flip_psum{cb}") for cb in range(CB)]
         flipped = [held.tile([P, KB, P], BF16, name=f"flipped{cb}") for cb in range(CB)]
         for cb in range(CB):
             for kb in range(KB):
-                nc.tensor.transpose(flip_psum[cb][:, kb, :], w_rows[cb][:, kb * P : (kb + 1) * P], identity[:])
+                nc.tensor.transpose(flip_psum[cb][:, kb, :], w_rows[:, cb, kb * P : (kb + 1) * P], identity[:])
         nc.scalar.activation(flipped[0][:], flip_psum[0][:], COPY)
 
         sumsq = held.tile([P, CB], F32, name="sumsq")
         squares = held.tile([P, K], F32, name="squares")
         for cb in range(CB):
             nc.vector.scalar_tensor_tensor(
-                squares[:], w_rows[cb][:], 1.0, w_rows[cb][:], op0=MULT, op1=MULT, accum_out=sumsq[:, cb : cb + 1]
+                squares[:], w_rows[:, cb, :], 1.0, w_rows[:, cb, :], op0=MULT, op1=MULT, accum_out=sumsq[:, cb : cb + 1]
             )
         nc.vector.tensor_copy(flipped[1][:], flip_psum[1][:])
         norm = held.tile([P, CB], F32, name="norm")

@@ -27,33 +27,34 @@ def tile_relaxedrecursivedoralinear_kernel(tc, base, x, w, bias, mag, offs, out)
         identity = held.tile([P, P], BF16, name="identity")
         make_identity(nc, identity[:])
 
-        w_rows = held.tile([P, CB, K], BF16, name="w_rows")
-        nc.sync.dma_start(w_rows[:], w.rearrange("(cb p) k -> p cb k", p=P))
+        w_rows = [held.tile([P, K], BF16, name=f"w_rows{cb}") for cb in range(CB)]
+        for cb in range(CB):
+            nc.sync.dma_start(w_rows[cb][:], w[cb * P : (cb + 1) * P, :])
         x_rows = held.tile([P, KB, N], BF16, name="x_rows")
-        nc.scalar.dma_start(x_rows[:], x.rearrange("(kb p) n -> p kb n", p=P))
-        bias_cols = held.tile([P, CB], F32, name="bias_cols")
-        mag_cols = held.tile([P, CB], F32, name="mag_cols")
-        with nc.allow_non_contiguous_dma(reason="256 single float32 values, one to a partition and block"):
-            nc.sync.dma_start(mag_cols[:], mag.rearrange("(cb p) o -> p (cb o)", p=P))
-            nc.sync.dma_start(bias_cols[:], bias.rearrange("(cb p) o -> p (cb o)", p=P))
+        nc.sync.dma_start(x_rows[:], x.rearrange("(kb p) n -> p kb n", p=P))
         offsets = held.tile([P, N // 16], U16, name="offsets")
         nc.sync.dma_start(offsets[:], offs)
         windows = [held.tile([P, S], F32, name=f"window{cb}") for cb in range(CB)]
         for cb in range(CB):
             nc.sync.dma_start(windows[cb][:], base[cb * P : (cb + 1) * P, :])
+        bias_cols = held.tile([P, CB], F32, name="bias_cols")
+        mag_cols = held.tile([P, CB], F32, name="mag_cols")
+        with nc.allow_non_contiguous_dma(reason="256 single float32 values, one to a partition and block"):
+            nc.scalar.dma_start(mag_cols[:], mag.rearrange("(cb p) o -> p (cb o)", p=P))
+            nc.scalar.dma_start(bias_cols[:], bias.rearrange("(cb p) o -> p (cb o)", p=P))
 
         flip_psum = [psum.tile([P, KB, P], BF16, name=f"flip_psum{cb}") for cb in range(CB)]
         flipped = [held.tile([P, KB, P], BF16, name=f"flipped{cb}") for cb in range(CB)]
         for cb in range(CB):
             for kb in range(KB):
-                nc.tensor.transpose(flip_psum[cb][:, kb, :], w_rows[:, cb, kb * P : (kb + 1) * P], identity[:])
+                nc.tensor.transpose(flip_psum[cb][:, kb, :], w_rows[cb][:, kb * P : (kb + 1) * P], identity[:])
         nc.scalar.activation(flipped[0][:], flip_psum[0][:], COPY)
 
         sumsq = held.tile([P, CB], F32, name="sumsq")
         squares = held.tile([P, K], F32, name="squares")
         for cb in range(CB):
             nc.vector.scalar_tensor_tensor(
-                squares[:], w_rows[:, cb, :], 1.0, w_rows[:, cb, :], op0=MULT, op1=MULT, accum_out=sumsq[:, cb : cb + 1]
+                squares[:], w_rows[cb][:], 1.0, w_rows[cb][:], op0=MULT, op1=MULT, accum_out=sumsq[:, cb : cb + 1]
             )
         nc.vector.tensor_copy(flipped[1][:], flip_psum[1][:])
         norm = held.tile([P, CB], F32, name="norm")
@@ -75,6 +76,8 @@ def tile_relaxedrecursivedoralinear_kernel(tc, base, x, w, bias, mag, offs, out)
                 finished[cb][:], product[:], bias_cols[:, cb : cb + 1], gain[:, cb : cb + 1], op0=ADD, op1=MULT
             )
 
-        for cb in range(CB):
-            nc.scalar.activation(windows[cb][:].indirect(offsets[:]), finished[cb][:], COPY)
-            nc.sync.dma_start(out[cb * P : (cb + 1) * P, :], windows[cb][:])
+        nc.scalar.activation(windows[0][:].indirect(offsets[:]), finished[0][:], COPY)
+        nc.sync.dma_start(out[:P, :], windows[0][:])
+        nc.scalar.activation(windows[1][:].indirect(offsets[:]), finished[1][:], COPY)
+        nc.sync.dma_start(out[P:, : S // 2], windows[1][:, : S // 2])
+        nc.scalar.dma_start(out[P:, S // 2 :], windows[1][:, S // 2 :])

@@ -26,6 +26,8 @@ def tile_relaxedrecursivedoralinear_kernel(tc, base, x, w, bias, mag, offs, out)
 
         identity = held.tile([P, P], BF16, name="identity")
         make_identity(nc, identity[:])
+        identity_f32 = held.tile([2 * CB, 2 * CB], F32, name="identity_f32")
+        make_identity(nc, identity_f32[:])
 
         w_rows = [held.tile([P, K], BF16, name=f"w_rows{cb}") for cb in range(CB)]
         for cb in range(CB):
@@ -37,11 +39,9 @@ def tile_relaxedrecursivedoralinear_kernel(tc, base, x, w, bias, mag, offs, out)
         windows = [held.tile([P, S], F32, name=f"window{cb}") for cb in range(CB)]
         for cb in range(CB):
             nc.sync.dma_start(windows[cb][:], base[cb * P : (cb + 1) * P, :])
-        bias_cols = held.tile([P, CB], F32, name="bias_cols")
-        mag_cols = held.tile([P, CB], F32, name="mag_cols")
-        with nc.allow_non_contiguous_dma(reason="256 single float32 values, one to a partition and block"):
-            nc.scalar.dma_start(mag_cols[:], mag.rearrange("(cb p) o -> p (cb o)", p=P))
-            nc.scalar.dma_start(bias_cols[:], bias.rearrange("(cb p) o -> p (cb o)", p=P))
+        small_rows = held.tile([2 * CB, P], F32, name="small_rows")
+        nc.scalar.dma_start(small_rows[:CB, :], mag.rearrange("(cb p) o -> cb (p o)", p=P))
+        nc.scalar.dma_start(small_rows[CB:, :], bias.rearrange("(cb p) o -> cb (p o)", p=P))
 
         flip_psum = [psum.tile([P, KB, P], BF16, name=f"flip_psum{cb}") for cb in range(CB)]
         flipped = [held.tile([P, KB, P], BF16, name=f"flipped{cb}") for cb in range(CB)]
@@ -50,6 +50,11 @@ def tile_relaxedrecursivedoralinear_kernel(tc, base, x, w, bias, mag, offs, out)
                 nc.tensor.transpose(flip_psum[cb][:, kb, :], w_rows[cb][:, kb * P : (kb + 1) * P], identity[:])
         nc.scalar.activation(flipped[0][:], flip_psum[0][:], COPY)
 
+        small_psum = psum.tile([P, 2 * CB], F32, name="small_psum")
+        nc.tensor.matmul(small_psum[:], small_rows[:], identity_f32[:], start=True, stop=True)
+        small_cols = held.tile([P, 2 * CB], F32, name="small_cols")
+        mag_cols, bias_cols = small_cols[:, :CB], small_cols[:, CB:]
+
         sumsq = held.tile([P, CB], F32, name="sumsq")
         squares = held.tile([P, K], F32, name="squares")
         for cb in range(CB):
@@ -57,6 +62,7 @@ def tile_relaxedrecursivedoralinear_kernel(tc, base, x, w, bias, mag, offs, out)
                 squares[:], w_rows[cb][:], 1.0, w_rows[cb][:], op0=MULT, op1=MULT, accum_out=sumsq[:, cb : cb + 1]
             )
         nc.vector.tensor_copy(flipped[1][:], flip_psum[1][:])
+        nc.vector.tensor_copy(small_cols[:], small_psum[:])
         norm = held.tile([P, CB], F32, name="norm")
         nc.scalar.activation(norm[:], sumsq[:], SQRT)
         inv_norm = held.tile([P, CB], F32, name="inv_norm")
@@ -76,8 +82,6 @@ def tile_relaxedrecursivedoralinear_kernel(tc, base, x, w, bias, mag, offs, out)
                 finished[cb][:], product[:], bias_cols[:, cb : cb + 1], gain[:, cb : cb + 1], op0=ADD, op1=MULT
             )
 
-        nc.scalar.activation(windows[0][:].indirect(offsets[:]), finished[0][:], COPY)
-        nc.sync.dma_start(out[:P, :], windows[0][:])
-        nc.scalar.activation(windows[1][:].indirect(offsets[:]), finished[1][:], COPY)
-        nc.sync.dma_start(out[P:, : S // 2], windows[1][:, : S // 2])
-        nc.scalar.dma_start(out[P:, S // 2 :], windows[1][:, S // 2 :])
+        for cb in range(CB):
+            nc.scalar.activation(windows[cb][:].indirect(offsets[:]), finished[cb][:], COPY)
+            nc.sync.dma_start(out[cb * P : (cb + 1) * P, :], windows[cb][:])

@@ -24,16 +24,14 @@ def tile_relaxedrecursivedoralinear_kernel(tc, base, x, w, bias, mag, offs, out)
         for i in range(WARM_MATMULS):
             nc.tensor.matmul(warm_psum[:], zeros[:], zeros[:], start=True, stop=True)
 
-        identity = held.tile([P, P], BF16, name="identity")
+        identity = held.tile([P, P], F32, name="identity")
         make_identity(nc, identity[:])
-        identity_f32 = held.tile([2 * CB, 2 * CB], F32, name="identity_f32")
-        make_identity(nc, identity_f32[:])
 
         w_rows = [held.tile([P, K], BF16, name=f"w_rows{cb}") for cb in range(CB)]
         for cb in range(CB):
             nc.sync.dma_start(w_rows[cb][:], w[cb * P : (cb + 1) * P, :])
         x_rows = held.tile([P, KB, N], BF16, name="x_rows")
-        nc.sync.dma_start(x_rows[:], x.rearrange("(kb p) n -> p kb n", p=P))
+        nc.sync.dma_start(x_rows[:], x.rearrange("(p half) n -> p half n", half=KB))
         offsets = held.tile([P, N // 16], U16, name="offsets")
         nc.sync.dma_start(offsets[:], offs)
         windows = [held.tile([P, S], F32, name=f"window{cb}") for cb in range(CB)]
@@ -43,43 +41,40 @@ def tile_relaxedrecursivedoralinear_kernel(tc, base, x, w, bias, mag, offs, out)
         nc.scalar.dma_start(small_rows[:CB, :], mag.rearrange("(cb p) o -> cb (p o)", p=P))
         nc.scalar.dma_start(small_rows[CB:, :], bias.rearrange("(cb p) o -> cb (p o)", p=P))
 
-        flip_psum = [psum.tile([P, KB, P], BF16, name=f"flip_psum{cb}") for cb in range(CB)]
-        flipped = [held.tile([P, KB, P], BF16, name=f"flipped{cb}") for cb in range(CB)]
-        for cb in range(CB):
-            for kb in range(KB):
-                nc.tensor.transpose(flip_psum[cb][:, kb, :], w_rows[cb][:, kb * P : (kb + 1) * P], identity[:])
-        nc.scalar.activation(flipped[0][:], flip_psum[0][:], COPY)
-
-        small_psum = psum.tile([P, 2 * CB], F32, name="small_psum")
-        nc.tensor.matmul(small_psum[:], small_rows[:], identity_f32[:], start=True, stop=True)
-        small_cols = held.tile([P, 2 * CB], F32, name="small_cols")
-        mag_cols, bias_cols = small_cols[:, :CB], small_cols[:, CB:]
-
-        sumsq = held.tile([P, CB], F32, name="sumsq")
+        flipped = [held.tile([P, P, KB], BF16, name=f"flipped{cb}") for cb in range(CB)]
+        sumsq = [held.tile([P, 1], F32, name=f"sumsq{cb}") for cb in range(CB)]
         squares = held.tile([P, K], F32, name="squares")
         for cb in range(CB):
+            words = psum.tile([P, P], F32, name=f"words{cb}")
+            nc.tensor.transpose(words[:], w_rows[cb][:].bitcast(F32), identity[:])
             nc.vector.scalar_tensor_tensor(
-                squares[:], w_rows[cb][:], 1.0, w_rows[cb][:], op0=MULT, op1=MULT, accum_out=sumsq[:, cb : cb + 1]
+                squares[:], w_rows[cb][:], 1.0, w_rows[cb][:], op0=MULT, op1=MULT, accum_out=sumsq[cb][:]
             )
-        nc.vector.tensor_copy(flipped[1][:], flip_psum[1][:])
+            nc.vector.tensor_copy(flipped[cb][:].rearrange("p c half -> p (c half)").bitcast(F32), words[:])
+
+        small_psum = psum.tile([P, 2 * CB], F32, name="small_psum")
+        nc.tensor.matmul(small_psum[:], small_rows[:], identity[: 2 * CB, : 2 * CB], start=True, stop=True)
+        small_cols = held.tile([P, 2 * CB], F32, name="small_cols")
+        mag_cols, bias_cols = small_cols[:, :CB], small_cols[:, CB:]
         nc.vector.tensor_copy(small_cols[:], small_psum[:])
-        norm = held.tile([P, CB], F32, name="norm")
-        nc.scalar.activation(norm[:], sumsq[:], SQRT)
-        inv_norm = held.tile([P, CB], F32, name="inv_norm")
-        nc.vector.reciprocal(inv_norm[:], norm[:])
-        gain = held.tile([P, CB], F32, name="gain")
+
+        gain = [held.tile([P, 1], F32, name=f"gain{cb}") for cb in range(CB)]
         for cb in range(CB):
-            nc.vector.tensor_scalar(
-                gain[:, cb : cb + 1], inv_norm[:, cb : cb + 1], mag_cols[:, cb : cb + 1], -1.0, op0=MULT, op1=ADD
-            )
+            norm = held.tile([P, 1], F32, name=f"norm{cb}")
+            nc.scalar.activation(norm[:], sumsq[cb][:], SQRT)
+            inv_norm = held.tile([P, 1], F32, name=f"inv_norm{cb}")
+            nc.vector.reciprocal(inv_norm[:], norm[:])
+            nc.vector.tensor_scalar(gain[cb][:], inv_norm[:], mag_cols[:, cb : cb + 1], -1.0, op0=MULT, op1=ADD)
 
         finished = [held.tile([P, N], F32, name=f"finished{cb}") for cb in range(CB)]
         for cb in range(CB):
             product = psum.tile([P, N], F32, name=f"product{cb}")
-            for kb in range(KB):
-                nc.tensor.matmul(product[:], flipped[cb][:, kb, :], x_rows[:, kb, :], start=kb == 0, stop=kb == KB - 1)
+            for half in range(KB):
+                nc.tensor.matmul(
+                    product[:], flipped[cb][:, :, half], x_rows[:, half, :], start=half == 0, stop=half == KB - 1
+                )
             nc.vector.tensor_scalar(
-                finished[cb][:], product[:], bias_cols[:, cb : cb + 1], gain[:, cb : cb + 1], op0=ADD, op1=MULT
+                finished[cb][:], product[:], bias_cols[:, cb : cb + 1], gain[cb][:], op0=ADD, op1=MULT
             )
 
         for cb in range(CB):

@@ -4,11 +4,14 @@ from concourse.masks import make_identity
 P = 128
 C, K, S, N = 256, 256, 512, 256
 CB = C // P
-KB = K // P
+HALVES = K // P
+SQUARE = 32
+GROUPS = P // SQUARE
+GK = K // GROUPS
 FLOPS = 2 * C * K * N
 
 BF16, F32, U16 = mybir.dt.bfloat16, mybir.dt.float32, mybir.dt.uint16
-ADD, MULT = mybir.AluOpType.add, mybir.AluOpType.mult
+ADD, MULT, POW = mybir.AluOpType.add, mybir.AluOpType.mult, mybir.AluOpType.pow
 COPY, SQRT = mybir.ActivationFunctionType.Copy, mybir.ActivationFunctionType.Sqrt
 
 WARM_MATMULS = 18
@@ -24,59 +27,73 @@ def tile_relaxedrecursivedoralinear_kernel(tc, base, x, w, bias, mag, offs, out)
         for i in range(WARM_MATMULS):
             nc.tensor.matmul(warm_psum[:], zeros[:], zeros[:], start=True, stop=True)
 
+        w_rows = held.tile([P, CB, K], BF16, name="w_rows")
+        nc.sync.dma_start(w_rows[:], w.rearrange("(p t) k -> p t k", t=CB))
+        grouped = held.tile([P, GROUPS * GK], BF16, name="grouped", align_bytes=64)
+        w_grouped = w.rearrange("(b j t) k -> t j b k", j=SQUARE, t=CB)
+        for a, queue in enumerate((nc.scalar, nc.scalar, nc.sync, nc.sync)):
+            rows = grouped[a * SQUARE : (a + 1) * SQUARE, :].rearrange("j (b k) -> j b k", b=GROUPS)
+            queue.dma_start(rows, w_grouped[0, :, :, a * GK : (a + 1) * GK])
+        x_rows = held.tile([P, HALVES, N], BF16, name="x_rows")
+        nc.sync.dma_start(x_rows[:], x.rearrange("(p half) n -> p half n", half=HALVES))
+        mag_cols = held.tile([P, CB], F32, name="mag_cols")
+        nc.scalar.dma_start(mag_cols[:], mag.rearrange("(p t) o -> p (t o)", t=CB))
+        bias_cols = held.tile([P, CB], F32, name="bias_cols")
+        nc.gpsimd.dma_start(bias_cols[:], bias.rearrange("(p t) o -> p (t o)", t=CB))
+        windows = [held.tile([P, S], F32, name=f"window{cb}") for cb in range(CB)]
+        base_rows = base.rearrange("(p t) s -> p t s", t=CB)
+        offsets = held.tile([P, N // 16], U16, name="offsets")
+        nc.sync.dma_start(windows[0][:], base_rows[:, 0, :])
+        nc.sync.dma_start(offsets[:], offs)
+        nc.sync.dma_start(windows[1][:], base_rows[:, 1, :])
         identity = held.tile([P, P], F32, name="identity")
         make_identity(nc, identity[:])
 
-        w_rows = [held.tile([P, K], BF16, name=f"w_rows{cb}") for cb in range(CB)]
-        for cb in range(CB):
-            nc.sync.dma_start(w_rows[cb][:], w[cb * P : (cb + 1) * P, :])
-        x_rows = held.tile([P, KB, N], BF16, name="x_rows")
-        nc.sync.dma_start(x_rows[:], x.rearrange("(p half) n -> p half n", half=KB))
-        offsets = held.tile([P, N // 16], U16, name="offsets")
-        nc.sync.dma_start(offsets[:], offs)
-        windows = [held.tile([P, S], F32, name=f"window{cb}") for cb in range(CB)]
-        for cb in range(CB):
-            nc.sync.dma_start(windows[cb][:], base[cb * P : (cb + 1) * P, :])
-        small_rows = held.tile([2 * CB, P], F32, name="small_rows")
-        nc.scalar.dma_start(small_rows[:CB, :], mag.rearrange("(cb p) o -> cb (p o)", p=P))
-        nc.scalar.dma_start(small_rows[CB:, :], bias.rearrange("(cb p) o -> cb (p o)", p=P))
-
-        flipped = [held.tile([P, P, KB], BF16, name=f"flipped{cb}") for cb in range(CB)]
-        sumsq = [held.tile([P, 1], F32, name=f"sumsq{cb}") for cb in range(CB)]
-        squares = held.tile([P, K], F32, name="squares")
-        for cb in range(CB):
-            words = psum.tile([P, P], F32, name=f"words{cb}")
-            nc.tensor.transpose(words[:], w_rows[cb][:].bitcast(F32), identity[:])
+        def sum_of_squares(cb, squares):
+            sumsq = held.tile([P, 1], F32, name=f"sumsq{cb}")
             nc.vector.scalar_tensor_tensor(
-                squares[:], w_rows[cb][:], 1.0, w_rows[cb][:], op0=MULT, op1=MULT, accum_out=sumsq[cb][:]
+                squares[:], w_rows[:, cb, :], 1.0, w_rows[:, cb, :], op0=MULT, op1=MULT, accum_out=sumsq[:]
             )
-            nc.vector.tensor_copy(flipped[cb][:].rearrange("p c half -> p (c half)").bitcast(F32), words[:])
+            return sumsq
 
-        small_psum = psum.tile([P, 2 * CB], F32, name="small_psum")
-        nc.tensor.matmul(small_psum[:], small_rows[:], identity[: 2 * CB, : 2 * CB], start=True, stop=True)
-        small_cols = held.tile([P, 2 * CB], F32, name="small_cols")
-        mag_cols, bias_cols = small_cols[:, :CB], small_cols[:, CB:]
-        nc.vector.tensor_copy(small_cols[:], small_psum[:])
-
-        gain = [held.tile([P, 1], F32, name=f"gain{cb}") for cb in range(CB)]
-        for cb in range(CB):
-            norm = held.tile([P, 1], F32, name=f"norm{cb}")
-            nc.scalar.activation(norm[:], sumsq[cb][:], SQRT)
-            inv_norm = held.tile([P, 1], F32, name=f"inv_norm{cb}")
-            nc.vector.reciprocal(inv_norm[:], norm[:])
-            nc.vector.tensor_scalar(gain[cb][:], inv_norm[:], mag_cols[:, cb : cb + 1], -1.0, op0=MULT, op1=ADD)
-
-        finished = [held.tile([P, N], F32, name=f"finished{cb}") for cb in range(CB)]
-        for cb in range(CB):
+        def multiply(cb, flipped):
             product = psum.tile([P, N], F32, name=f"product{cb}")
-            for half in range(KB):
+            for half in range(HALVES):
                 nc.tensor.matmul(
-                    product[:], flipped[cb][:, :, half], x_rows[:, half, :], start=half == 0, stop=half == KB - 1
+                    product[:], flipped[:, half::HALVES], x_rows[:, half, :], start=half == 0, stop=half == HALVES - 1
                 )
-            nc.vector.tensor_scalar(
-                finished[cb][:], product[:], bias_cols[:, cb : cb + 1], gain[cb][:], op0=ADD, op1=MULT
-            )
+            return product
 
-        for cb in range(CB):
-            nc.scalar.activation(windows[cb][:].indirect(offsets[:]), finished[cb][:], COPY)
-            nc.sync.dma_start(out[cb * P : (cb + 1) * P, :], windows[cb][:])
+        def finish(cb, product, gain):
+            finished = held.tile([P, N], F32, name=f"finished{cb}")
+            nc.vector.tensor_scalar(finished[:], product[:], bias_cols[:, cb : cb + 1], gain[:], op0=ADD, op1=MULT)
+            return finished
+
+        def place(cb, finished):
+            nc.scalar.activation(windows[cb][:].indirect(offsets[:]), finished[:], COPY)
+            nc.sync.dma_start(out.rearrange("(p t) s -> p t s", t=CB)[:, cb, :], windows[cb][:])
+
+        sumsq0 = sum_of_squares(0, held.tile([P, K], BF16, name="squares0"))
+        flipped0 = held.tile([P, P * HALVES], BF16, name="flipped0", align_bytes=64)
+        nc.vector.transpose(flipped0[:].bitcast(F32), grouped[:].bitcast(F32))
+        product0 = multiply(0, flipped0)
+        norm0 = held.tile([P, 1], F32, name="norm0")
+        nc.scalar.activation(norm0[:], sumsq0[:], SQRT)
+        inv_norm0 = held.tile([P, 1], F32, name="inv_norm0")
+        nc.vector.reciprocal(inv_norm0[:], norm0[:])
+        gain0 = held.tile([P, 1], F32, name="gain0")
+        nc.vector.tensor_scalar(gain0[:], inv_norm0[:], mag_cols[:, 0:1], -1.0, op0=MULT, op1=ADD)
+        place(0, finish(0, product0, gain0))
+
+        sumsq1 = sum_of_squares(1, held.tile([P, K], BF16, name="squares1", tag="grouped", align_bytes=64))
+        minus_half = held.tile([P, 1], F32, name="minus_half")
+        nc.gpsimd.memset(minus_half[:], -0.5)
+        inv_norm1 = held.tile([P, 1], F32, name="inv_norm1")
+        nc.gpsimd.tensor_tensor(inv_norm1[:], sumsq1[:], minus_half[:], POW)
+        gain1 = held.tile([P, 1], F32, name="gain1")
+        nc.gpsimd.tensor_scalar(gain1[:], inv_norm1[:], mag_cols[:, 1:2], -1.0, op0=MULT, op1=ADD)
+        words1 = psum.tile([P, P], F32, name="words1")
+        nc.tensor.transpose(words1[:], w_rows[:, 1, :].bitcast(F32), identity[:])
+        flipped1 = held.tile([P, P * HALVES], BF16, name="flipped1")
+        nc.scalar.copy(flipped1[:].bitcast(F32), words1[:])
+        place(1, finish(1, multiply(1, flipped1), gain1))

@@ -31,13 +31,13 @@ def tile_relaxedrecursivedoralinear_kernel(tc, base, x, w, bias, mag, offs, out)
         nc.sync.dma_start(w_rows[:], w.rearrange("(p t) k -> p t k", t=CB))
         grouped = held.tile([P, GROUPS * GK], BF16, name="grouped", align_bytes=64)
         w_grouped = w.rearrange("(b j t) k -> t j b k", j=SQUARE, t=CB)
-        for a, queue in enumerate((nc.scalar, nc.scalar, nc.sync, nc.sync)):
+        for a in range(GROUPS):
             rows = grouped[a * SQUARE : (a + 1) * SQUARE, :].rearrange("j (b k) -> j b k", b=GROUPS)
-            queue.dma_start(rows, w_grouped[0, :, :, a * GK : (a + 1) * GK])
+            nc.sync.dma_start(rows, w_grouped[0, :, :, a * GK : (a + 1) * GK])
         x_rows = held.tile([P, HALVES, N], BF16, name="x_rows")
         nc.sync.dma_start(x_rows[:], x.rearrange("(p half) n -> p half n", half=HALVES))
         mag_cols = held.tile([P, CB], F32, name="mag_cols")
-        nc.scalar.dma_start(mag_cols[:], mag.rearrange("(p t) o -> p (t o)", t=CB))
+        nc.sync.dma_start(mag_cols[:], mag.rearrange("(p t) o -> p (t o)", t=CB))
         bias_cols = held.tile([P, CB], F32, name="bias_cols")
         nc.gpsimd.dma_start(bias_cols[:], bias.rearrange("(p t) o -> p (t o)", t=CB))
         windows = [held.tile([P, S], F32, name=f"window{cb}") for cb in range(CB)]
@@ -83,7 +83,7 @@ def tile_relaxedrecursivedoralinear_kernel(tc, base, x, w, bias, mag, offs, out)
         nc.vector.reciprocal(inv_norm0[:], norm0[:])
         gain0 = held.tile([P, 1], F32, name="gain0")
         nc.vector.tensor_scalar(gain0[:], inv_norm0[:], mag_cols[:, 0:1], -1.0, op0=MULT, op1=ADD)
-        place(0, finish(0, product0, gain0))
+        finished0 = finish(0, product0, gain0)
 
         sumsq1 = sum_of_squares(1, held.tile([P, K], BF16, name="squares1", tag="grouped", align_bytes=64))
         minus_half = held.tile([P, 1], F32, name="minus_half")
@@ -95,5 +95,8 @@ def tile_relaxedrecursivedoralinear_kernel(tc, base, x, w, bias, mag, offs, out)
         words1 = psum.tile([P, P], F32, name="words1")
         nc.tensor.transpose(words1[:], w_rows[:, 1, :].bitcast(F32), identity[:])
         flipped1 = held.tile([P, P * HALVES], BF16, name="flipped1")
-        nc.scalar.copy(flipped1[:].bitcast(F32), words1[:])
-        place(1, finish(1, multiply(1, flipped1), gain1))
+        nc.vector.tensor_copy(flipped1[:].bitcast(F32), words1[:])
+        finished1 = finish(1, multiply(1, flipped1), gain1)
+
+        place(0, finished0)
+        place(1, finished1)

@@ -5,16 +5,15 @@ P = 128
 C, K, S, N = 256, 256, 512, 256
 CB = C // P
 HALVES = K // P
-SQUARE = 32
-GROUPS = P // SQUARE
-GK = K // GROUPS
+PIECES = 2
+TOKENS = N // PIECES
 FLOPS = 2 * C * K * N
 
 BF16, F32, U16 = mybir.dt.bfloat16, mybir.dt.float32, mybir.dt.uint16
 ADD, MULT, POW = mybir.AluOpType.add, mybir.AluOpType.mult, mybir.AluOpType.pow
 COPY, SQRT = mybir.ActivationFunctionType.Copy, mybir.ActivationFunctionType.Sqrt
 
-WARM_MATMULS = 18
+WARM_MATMULS = 14
 
 
 def tile_relaxedrecursivedoralinear_kernel(tc, base, x, w, bias, mag, offs, out):
@@ -27,56 +26,66 @@ def tile_relaxedrecursivedoralinear_kernel(tc, base, x, w, bias, mag, offs, out)
         for i in range(WARM_MATMULS):
             nc.tensor.matmul(warm_psum[:], zeros[:], zeros[:], start=True, stop=True)
 
-        w_rows = held.tile([P, CB, K], BF16, name="w_rows")
-        nc.sync.dma_start(w_rows[:], w.rearrange("(p t) k -> p t k", t=CB))
-        grouped = held.tile([P, GROUPS * GK], BF16, name="grouped", align_bytes=64)
-        w_grouped = w.rearrange("(b j t) k -> t j b k", j=SQUARE, t=CB)
-        for a in range(GROUPS):
-            rows = grouped[a * SQUARE : (a + 1) * SQUARE, :].rearrange("j (b k) -> j b k", b=GROUPS)
-            nc.sync.dma_start(rows, w_grouped[0, :, :, a * GK : (a + 1) * GK])
+        w_rows = [held.tile([P, K], BF16, name=f"w_rows{cb}") for cb in range(CB)]
+        for cb in range(CB):
+            nc.sync.dma_start(w_rows[cb][:], w.rearrange("(p t) k -> p t k", t=CB)[:, cb, :])
         x_rows = held.tile([P, HALVES, N], BF16, name="x_rows")
         nc.sync.dma_start(x_rows[:], x.rearrange("(p half) n -> p half n", half=HALVES))
         mag_cols = held.tile([P, CB], F32, name="mag_cols")
         nc.sync.dma_start(mag_cols[:], mag.rearrange("(p t) o -> p (t o)", t=CB))
         bias_cols = held.tile([P, CB], F32, name="bias_cols")
-        nc.gpsimd.dma_start(bias_cols[:], bias.rearrange("(p t) o -> p (t o)", t=CB))
-        windows = [held.tile([P, S], F32, name=f"window{cb}") for cb in range(CB)]
-        base_rows = base.rearrange("(p t) s -> p t s", t=CB)
+        nc.sync.dma_start(bias_cols[:], bias.rearrange("(p t) o -> p (t o)", t=CB))
         offsets = held.tile([P, N // 16], U16, name="offsets")
-        nc.sync.dma_start(windows[0][:], base_rows[:, 0, :])
         nc.sync.dma_start(offsets[:], offs)
-        nc.sync.dma_start(windows[1][:], base_rows[:, 1, :])
+        windows = [held.tile([P, S], F32, name=f"window{cb}") for cb in range(CB)]
+        for cb in range(CB):
+            nc.sync.dma_start(windows[cb][:], base.rearrange("(p t) s -> p t s", t=CB)[:, cb, :])
         identity = held.tile([P, P], F32, name="identity")
         make_identity(nc, identity[:])
 
-        def sum_of_squares(cb, squares):
+        def sum_of_squares(cb):
             sumsq = held.tile([P, 1], F32, name=f"sumsq{cb}")
+            squares = held.tile([P, K], BF16, name=f"squares{cb}")
             nc.vector.scalar_tensor_tensor(
-                squares[:], w_rows[:, cb, :], 1.0, w_rows[:, cb, :], op0=MULT, op1=MULT, accum_out=sumsq[:]
+                squares[:], w_rows[cb][:], 1.0, w_rows[cb][:], op0=MULT, op1=MULT, accum_out=sumsq[:]
             )
             return sumsq
 
-        def multiply(cb, flipped):
-            product = psum.tile([P, N], F32, name=f"product{cb}")
-            for half in range(HALVES):
-                nc.tensor.matmul(
-                    product[:], flipped[:, half::HALVES], x_rows[:, half, :], start=half == 0, stop=half == HALVES - 1
-                )
-            return product
+        def flip(cb, copy):
+            words = psum.tile([P, P], F32, name=f"words{cb}")
+            nc.tensor.transpose(words[:], w_rows[cb][:].bitcast(F32), identity[:])
+            flipped = held.tile([P, P * HALVES], BF16, name=f"flipped{cb}")
+            copy(flipped[:].bitcast(F32), words[:])
+            return flipped
 
-        def finish(cb, product, gain):
+        def multiply(cb, flipped):
+            pieces = []
+            for piece in range(PIECES):
+                product = psum.tile([P, TOKENS], F32, name=f"product{cb}_{piece}", tag=f"product{piece}")
+                tokens = slice(piece * TOKENS, (piece + 1) * TOKENS)
+                for half in range(HALVES):
+                    nc.tensor.matmul(
+                        product[:], flipped[:, half::HALVES], x_rows[:, half, tokens],
+                        start=half == 0, stop=half == HALVES - 1,
+                    )
+                pieces.append(product)
+            return pieces
+
+        def finish(cb, pieces, gain):
             finished = held.tile([P, N], F32, name=f"finished{cb}")
-            nc.vector.tensor_scalar(finished[:], product[:], bias_cols[:, cb : cb + 1], gain[:], op0=ADD, op1=MULT)
+            for piece, product in enumerate(pieces):
+                tokens = slice(piece * TOKENS, (piece + 1) * TOKENS)
+                nc.vector.tensor_scalar(
+                    finished[:, tokens], product[:], bias_cols[:, cb : cb + 1], gain[:], op0=ADD, op1=MULT
+                )
             return finished
 
         def place(cb, finished):
             nc.scalar.activation(windows[cb][:].indirect(offsets[:]), finished[:], COPY)
             nc.sync.dma_start(out.rearrange("(p t) s -> p t s", t=CB)[:, cb, :], windows[cb][:])
 
-        sumsq0 = sum_of_squares(0, held.tile([P, K], BF16, name="squares0"))
-        flipped0 = held.tile([P, P * HALVES], BF16, name="flipped0", align_bytes=64)
-        nc.vector.transpose(flipped0[:].bitcast(F32), grouped[:].bitcast(F32))
-        product0 = multiply(0, flipped0)
+        sumsq0 = sum_of_squares(0)
+        product0 = multiply(0, flip(0, nc.scalar.copy))
         norm0 = held.tile([P, 1], F32, name="norm0")
         nc.scalar.activation(norm0[:], sumsq0[:], SQRT)
         inv_norm0 = held.tile([P, 1], F32, name="inv_norm0")
@@ -85,18 +94,15 @@ def tile_relaxedrecursivedoralinear_kernel(tc, base, x, w, bias, mag, offs, out)
         nc.vector.tensor_scalar(gain0[:], inv_norm0[:], mag_cols[:, 0:1], -1.0, op0=MULT, op1=ADD)
         finished0 = finish(0, product0, gain0)
 
-        sumsq1 = sum_of_squares(1, held.tile([P, K], BF16, name="squares1", tag="grouped", align_bytes=64))
+        sumsq1 = sum_of_squares(1)
+        product1 = multiply(1, flip(1, nc.vector.tensor_copy))
         minus_half = held.tile([P, 1], F32, name="minus_half")
         nc.gpsimd.memset(minus_half[:], -0.5)
         inv_norm1 = held.tile([P, 1], F32, name="inv_norm1")
         nc.gpsimd.tensor_tensor(inv_norm1[:], sumsq1[:], minus_half[:], POW)
         gain1 = held.tile([P, 1], F32, name="gain1")
         nc.gpsimd.tensor_scalar(gain1[:], inv_norm1[:], mag_cols[:, 1:2], -1.0, op0=MULT, op1=ADD)
-        words1 = psum.tile([P, P], F32, name="words1")
-        nc.tensor.transpose(words1[:], w_rows[:, 1, :].bitcast(F32), identity[:])
-        flipped1 = held.tile([P, P * HALVES], BF16, name="flipped1")
-        nc.vector.tensor_copy(flipped1[:].bitcast(F32), words1[:])
-        finished1 = finish(1, multiply(1, flipped1), gain1)
+        finished1 = finish(1, product1, gain1)
 
         place(0, finished0)
         place(1, finished1)

@@ -26,6 +26,7 @@ def tile_relaxedrecursivedoralinear_kernel(tc, base, x, w, bias, mag, offs, out)
         for i in range(WARM_MATMULS):
             nc.tensor.matmul(warm_psum[:], zeros[:], zeros[:], start=True, stop=True)
 
+        quarters = [slice(q * P // 4, (q + 1) * P // 4) for q in range(4)]
         w_rows = [held.tile([P, K], BF16, name=f"w_rows{cb}") for cb in range(CB)]
         for cb in range(CB):
             nc.sync.dma_start(w_rows[cb][:], w.rearrange("(p t) k -> p t k", t=CB)[:, cb, :])
@@ -38,8 +39,10 @@ def tile_relaxedrecursivedoralinear_kernel(tc, base, x, w, bias, mag, offs, out)
         offsets = held.tile([P, N // 16], U16, name="offsets")
         nc.sync.dma_start(offsets[:], offs)
         windows = [held.tile([P, S], F32, name=f"window{cb}") for cb in range(CB)]
-        for cb in range(CB):
-            nc.sync.dma_start(windows[cb][:], base.rearrange("(p t) s -> p t s", t=CB)[:, cb, :])
+        base_rows = base.rearrange("(p t) s -> p t s", t=CB)
+        nc.sync.dma_start(windows[0][:], base_rows[:, 0, :])
+        for rows in quarters:
+            nc.sync.dma_start(windows[1][rows, :], base_rows[rows, 1, :])
         identity = held.tile([P, P], F32, name="identity")
         make_identity(nc, identity[:])
 
@@ -80,9 +83,10 @@ def tile_relaxedrecursivedoralinear_kernel(tc, base, x, w, bias, mag, offs, out)
                 )
             return finished
 
+        out_rows = out.rearrange("(p t) s -> p t s", t=CB)
+
         def place(cb, finished):
             nc.scalar.activation(windows[cb][:].indirect(offsets[:]), finished[:], COPY)
-            nc.sync.dma_start(out.rearrange("(p t) s -> p t s", t=CB)[:, cb, :], windows[cb][:])
 
         sumsq0 = sum_of_squares(0)
         product0 = multiply(0, flip(0, nc.scalar.copy))
@@ -105,4 +109,7 @@ def tile_relaxedrecursivedoralinear_kernel(tc, base, x, w, bias, mag, offs, out)
         finished1 = finish(1, product1, gain1)
 
         place(0, finished0)
+        for rows in quarters:
+            nc.sync.dma_start(out_rows[rows, 0, :], windows[0][rows, :])
         place(1, finished1)
+        nc.sync.dma_start(out_rows[:, 1, :], windows[1][:])

@@ -5,7 +5,7 @@ P = 128
 C, K, S, N = 256, 256, 512, 256
 CB = C // P
 HALVES = K // P
-PIECES = 2
+PIECES = 4
 TOKENS = N // PIECES
 FLOPS = 2 * C * K * N
 
@@ -13,7 +13,7 @@ BF16, F32, U16 = mybir.dt.bfloat16, mybir.dt.float32, mybir.dt.uint16
 ADD, MULT, POW = mybir.AluOpType.add, mybir.AluOpType.mult, mybir.AluOpType.pow
 COPY, SQRT = mybir.ActivationFunctionType.Copy, mybir.ActivationFunctionType.Sqrt
 
-WARM_MATMULS = 14
+WARM_MATMULS = 8
 
 
 def tile_relaxedrecursivedoralinear_kernel(tc, base, x, w, bias, mag, offs, out):

import concourse.mybir as mybir
from concourse.masks import make_identity

P = 128
C, K, S, N = 256, 256, 512, 256
CB = C // P
HALVES = K // P
PIECES = 4
TOKENS = N // PIECES
FLOPS = 2 * C * K * N

BF16, F32, U16 = mybir.dt.bfloat16, mybir.dt.float32, mybir.dt.uint16
ADD, MULT, POW = mybir.AluOpType.add, mybir.AluOpType.mult, mybir.AluOpType.pow
COPY, SQRT = mybir.ActivationFunctionType.Copy, mybir.ActivationFunctionType.Sqrt

WARM_MATMULS = 8


def tile_relaxedrecursivedoralinear_kernel(tc, base, x, w, bias, mag, offs, out):
    nc = tc.nc
    with tc.tile_pool(name="held", bufs=1) as held, tc.psum_pool(name="psum", bufs=1) as psum:

        zeros = held.tile([P, P], BF16, name="zeros")
        nc.gpsimd.memset(zeros[:], 0.0)
        warm_psum = psum.tile([P, P], F32, name="warm_psum")
        for i in range(WARM_MATMULS):
            nc.tensor.matmul(warm_psum[:], zeros[:], zeros[:], start=True, stop=True)

        quarters = [slice(q * P // 4, (q + 1) * P // 4) for q in range(4)]
        w_rows = [held.tile([P, K], BF16, name=f"w_rows{cb}") for cb in range(CB)]
        for cb in range(CB):
            nc.sync.dma_start(w_rows[cb][:], w.rearrange("(p t) k -> p t k", t=CB)[:, cb, :])
        x_rows = held.tile([P, HALVES, N], BF16, name="x_rows")
        nc.sync.dma_start(x_rows[:], x.rearrange("(p half) n -> p half n", half=HALVES))
        mag_cols = held.tile([P, CB], F32, name="mag_cols")
        nc.sync.dma_start(mag_cols[:], mag.rearrange("(p t) o -> p (t o)", t=CB))
        bias_cols = held.tile([P, CB], F32, name="bias_cols")
        nc.sync.dma_start(bias_cols[:], bias.rearrange("(p t) o -> p (t o)", t=CB))
        offsets = held.tile([P, N // 16], U16, name="offsets")
        nc.sync.dma_start(offsets[:], offs)
        windows = [held.tile([P, S], F32, name=f"window{cb}") for cb in range(CB)]
        base_rows = base.rearrange("(p t) s -> p t s", t=CB)
        nc.sync.dma_start(windows[0][:], base_rows[:, 0, :])
        for rows in quarters:
            nc.sync.dma_start(windows[1][rows, :], base_rows[rows, 1, :])
        identity = held.tile([P, P], F32, name="identity")
        make_identity(nc, identity[:])

        def sum_of_squares(cb):
            sumsq = held.tile([P, 1], F32, name=f"sumsq{cb}")
            squares = held.tile([P, K], BF16, name=f"squares{cb}")
            nc.vector.scalar_tensor_tensor(
                squares[:], w_rows[cb][:], 1.0, w_rows[cb][:], op0=MULT, op1=MULT, accum_out=sumsq[:]
            )
            return sumsq

        def flip(cb, copy):
            words = psum.tile([P, P], F32, name=f"words{cb}")
            nc.tensor.transpose(words[:], w_rows[cb][:].bitcast(F32), identity[:])
            flipped = held.tile([P, P * HALVES], BF16, name=f"flipped{cb}")
            copy(flipped[:].bitcast(F32), words[:])
            return flipped

        def multiply(cb, flipped):
            pieces = []
            for piece in range(PIECES):
                product = psum.tile([P, TOKENS], F32, name=f"product{cb}_{piece}", tag=f"product{piece}")
                tokens = slice(piece * TOKENS, (piece + 1) * TOKENS)
                for half in range(HALVES):
                    nc.tensor.matmul(
                        product[:], flipped[:, half::HALVES], x_rows[:, half, tokens],
                        start=half == 0, stop=half == HALVES - 1,
                    )
                pieces.append(product)
            return pieces

        def finish(cb, pieces, gain):
            finished = held.tile([P, N], F32, name=f"finished{cb}")
            for piece, product in enumerate(pieces):
                tokens = slice(piece * TOKENS, (piece + 1) * TOKENS)
                nc.vector.tensor_scalar(
                    finished[:, tokens], product[:], bias_cols[:, cb : cb + 1], gain[:], op0=ADD, op1=MULT
                )
            return finished

        out_rows = out.rearrange("(p t) s -> p t s", t=CB)

        def place(cb, finished):
            nc.scalar.activation(windows[cb][:].indirect(offsets[:]), finished[:], COPY)

        sumsq0 = sum_of_squares(0)
        product0 = multiply(0, flip(0, nc.scalar.copy))
        norm0 = held.tile([P, 1], F32, name="norm0")
        nc.scalar.activation(norm0[:], sumsq0[:], SQRT)
        inv_norm0 = held.tile([P, 1], F32, name="inv_norm0")
        nc.vector.reciprocal(inv_norm0[:], norm0[:])
        gain0 = held.tile([P, 1], F32, name="gain0")
        nc.vector.tensor_scalar(gain0[:], inv_norm0[:], mag_cols[:, 0:1], -1.0, op0=MULT, op1=ADD)
        finished0 = finish(0, product0, gain0)

        sumsq1 = sum_of_squares(1)
        product1 = multiply(1, flip(1, nc.vector.tensor_copy))
        minus_half = held.tile([P, 1], F32, name="minus_half")
        nc.gpsimd.memset(minus_half[:], -0.5)
        inv_norm1 = held.tile([P, 1], F32, name="inv_norm1")
        nc.gpsimd.tensor_tensor(inv_norm1[:], sumsq1[:], minus_half[:], POW)
        gain1 = held.tile([P, 1], F32, name="gain1")
        nc.gpsimd.tensor_scalar(gain1[:], inv_norm1[:], mag_cols[:, 1:2], -1.0, op0=MULT, op1=ADD)
        finished1 = finish(1, product1, gain1)

        place(0, finished0)
        for rows in quarters:
            nc.sync.dma_start(out_rows[rows, 0, :], windows[0][rows, :])
        place(1, finished1)
        nc.sync.dma_start(out_rows[:, 1, :], windows[1][:])
